import numpy as np
import ml_dtypes


def mxq(x, axis, fmt="e4m3"):
    dtype, down = {"e4m3": (ml_dtypes.float8_e4m3fn, 7), "e5m2": (ml_dtypes.float8_e5m2, 14)}[fmt]
    v = np.moveaxis(np.asarray(x, np.float32).astype(ml_dtypes.bfloat16).astype(np.float64), axis, -1)
    blocks = v.reshape(v.shape[:-1] + (-1, 32))
    amax = np.abs(blocks).max(-1, keepdims=True)
    byte = np.maximum(np.where(amax > 0, np.frexp(amax)[1] - 1 + 127, 0) - down, 1)
    scale = np.exp2(byte - 127.0)
    codes = (blocks / scale).astype(np.float32).astype(dtype).astype(np.float64)
    return np.moveaxis((codes * scale).reshape(v.shape), -1, axis)


WIDE = False


def mx_kscale(k):
    if not WIDE:
        return np.ones(k)
    levels = np.array([18, -18])
    if k % 512:
        return np.exp2(np.random.permutation(np.resize(levels, k // 32))).repeat(32)
    a = np.empty((k // 512, 16))
    for p in range(k // 512):
        a[p, :8] = np.random.permutation(np.resize(levels, 8))
        for g in range(8):
            far = levels[np.abs(levels - a[p, g]) >= 10]
            a[p, g + 8] = far[np.random.randint(len(far))]
    return np.exp2(a.ravel()).repeat(32)


BF16 = ml_dtypes.bfloat16


def bf(x):
    return np.asarray(x, np.float32).astype(BF16)


def f64(x):
    return np.asarray(x).astype(np.float64)


B, N, F, L, R = 1024, 2048, 1024, 512, 16
SIGMA_ENC = 1.0
G_SCALE = 32.0


def near_subspace(rows, basis):
    out = np.random.standard_normal((rows, F)) * np.sqrt(0.5 / F)
    for p in basis:
        out = out + np.outer(np.random.standard_normal(rows), p) * np.sqrt(2.0 / R)
    return out


def rbf_gram(a, b, sigma):
    sq = np.sum(a * a, axis=-1)[:, None] + np.sum(b * b, axis=-1)[None, :] - 2.0 * (a @ b.T)
    sq = np.maximum(sq, 0.0)
    return np.exp(-sq / (2.0 * sigma * sigma))


def setup_inputs():
    u = mx_kscale(L)
    v = mx_kscale(N)
    v = v / v.max()
    s = mx_kscale(B)
    s = s / s.min()
    basis = np.random.standard_normal((R, F)) / np.sqrt(F)
    x0 = bf(near_subspace(B, basis))
    c0 = bf(near_subspace(N, basis))
    a0 = bf(np.random.standard_normal((L, N)) / np.sqrt(N))
    g = np.random.standard_normal((B, L)) * np.exp2(np.random.randint(-6, 1, (B, 1))) * G_SCALE
    k_enc = rbf_gram(f64(x0), f64(c0), SIGMA_ENC)
    return {"x": bf(f64(x0) * s[:, None]),
            "centers_encoder": bf(f64(c0) / v[:, None]),
            "alpha_encoder": bf(f64(a0) * v[None, :] / u[:, None]),
            "k_enc": np.asarray(k_enc, np.float32),
            "grad_out": bf(g / s[:, None] * u[None, :])}


def reference(x, centers_encoder, alpha_encoder, k_enc, grad_out):
    xf = f64(x)
    cf = f64(centers_encoder)
    dk = mxq(f64(grad_out), 1, "e5m2") @ mxq(f64(alpha_encoder), 0, "e4m3")
    ds = dk * f64(k_enc) / (SIGMA_ENC * SIGMA_ENC)
    row = np.sum(ds, axis=1)
    col = np.sum(ds, axis=0)
    dx = (mxq(ds, 1, "e5m2") @ mxq(cf, 0, "e4m3")) - xf * row[:, None]
    dc = (mxq(ds, 0, "e5m2").T @ mxq(xf, 0, "e4m3")) - cf * col[:, None]
    return dx, dc

@@ -1,0 +1,367 @@
+from contextlib import ExitStack
+
+import concourse.mybir as mybir
+from concourse.masks import make_identity
+
+B, N, F, L = 1024, 2048, 1024, 512
+FLOPS = 2 * B * N * L + 2 * (2 * B * N * F)
+
+F32 = mybir.dt.float32
+BF16 = mybir.dt.bfloat16
+U32 = mybir.dt.uint32
+U8 = mybir.dt.uint8
+E4 = mybir.dt.float8_e4m3fn_x4
+E5 = mybir.dt.float8_e5m2_x4
+MUL = mybir.AluOpType.mult
+ADD = mybir.AluOpType.add
+SUB = mybir.AluOpType.subtract
+AX = mybir.AxisListType.X
+
+P = 128
+NG = B // 512
+NH = N // 512
+
+UNITS = [(0, 0), (1, 0), (0, 1), (1, 1), (0, 2), (0, 3), (1, 2), (1, 3)]
+
+
+def tile_autoencoder_pa_v_kernel(tc, x, centers, alpha, k_enc, grad_out, out_0, out_1):
+    nc = tc.nc
+    x_v = x.rearrange("(g p j) f -> g p j f", g=NG, j=4)
+    c_v = centers.rearrange("(h p j) f -> h p j f", h=NH, j=4)
+    al_v = alpha.rearrange("(p j) n -> p j n", j=4)
+    k_v = k_enc.rearrange("(g p j) n -> g p j n", g=NG, j=4)
+    g_v = grad_out.rearrange("(g p j) l -> g p j l", g=NG, j=4)
+    dx_v = out_0.rearrange("(g p j) f -> g j p f", g=NG, j=4)
+    dc_v = out_1.rearrange("(h p j) f -> h j p f", h=NH, j=4)
+
+    with ExitStack() as ctx:
+        keep = ctx.enter_context(tc.tile_pool(name="keep", bufs=1))
+        stream = ctx.enter_context(tc.tile_pool(name="stream", bufs=2))
+        psum = ctx.enter_context(tc.psum_pool(name="psum", bufs=2))
+        ctx.enter_context(tc.manual_schedule())
+
+        def sb(name, shape, dtype):
+            return keep.tile(shape, dtype, name=name, align_bytes=64)
+
+        def st(tag, shape, dtype, bufs):
+            return stream.tile(shape, dtype, name=tag, tag=tag, bufs=bufs, align_bytes=64)
+
+        def bank(tag, bufs):
+            return psum.tile([P, 512], F32, name=tag, tag=tag, bufs=bufs)
+
+        ident = sb("ident", [P, P], F32)
+        make_identity(nc, ident[:])
+
+        x_raw = [sb(f"x_raw{g}", [P, 4, F], BF16) for g in range(NG)]
+        c_raw = [sb(f"c_raw{h}", [P, 4, F], BF16) for h in range(NH)]
+        x_q = [[(sb(f"xc{g}{f}", [P, 512], U32), sb(f"xs{g}{f}", [P, 512], U8)) for f in range(2)] for g in range(NG)]
+        c_q = [[(sb(f"cc{h}{f}", [P, 512], U32), sb(f"cs{h}{f}", [P, 512], U8)) for f in range(2)] for h in range(NH)]
+        al_q = [(sb(f"alc{h}", [P, 512], U32), sb(f"als{h}", [P, 512], U8)) for h in range(NH)]
+        g_q = [(sb(f"gc{g}", [P, 512], U32), sb(f"gs{g}", [P, 512], U8)) for g in range(NG)]
+        a_q = {u: (sb(f"ac{u[0]}{u[1]}", [P, 512], U32), sb(f"as{u[0]}{u[1]}", [P, 512], U8)) for u in UNITS}
+        b_q = {u: (sb(f"bc{u[0]}{u[1]}", [P, 512], U32), sb(f"bs{u[0]}{u[1]}", [P, 512], U8)) for u in UNITS}
+        row = sb("row", [P, NG, 4, NH], F32)
+        nrow = sb("nrow", [P, NG, 4], F32)
+        colp = sb("colp", [P, NG, NH, 4], F32)
+        ncol = sb("ncol", [P, NH, 4], F32)
+
+        raw = {}
+        k_t = {}
+        ds_t = {}
+        grp_t = {}
+        dk_b = {}
+        col_b = {}
+        mm_b = {}
+        out_t = {}
+
+        def load_g(g):
+            t = st("araw", [P, 4, 512], BF16, 3)
+            nc.sync.dma_start(out=t[:], in_=g_v[g])
+            raw[("g", g)] = t
+
+        def load_al(h):
+            t = st("araw", [P, 4, 512], BF16, 3)
+            nc.sync.dma_start(out=t[:], in_=al_v[:, :, 512 * h : 512 * (h + 1)])
+            raw[("al", h)] = t
+
+        def load_k(u, parts=1):
+            g, h = u
+            t = st("k", [P, 4, 512], F32, 3)
+            w = 4 // parts
+            for i in range(parts):
+                nc.sync.dma_start(out=t[:, w * i : w * (i + 1), :], in_=k_v[g, :, w * i : w * (i + 1), 512 * h : 512 * (h + 1)])
+            k_t[u] = t
+
+        def load_x(g):
+            nc.sync.dma_start(out=x_raw[g][:], in_=x_v[g])
+
+        def load_c(h):
+            nc.sync.dma_start(out=c_raw[h][:], in_=c_v[h])
+
+        def grp(key):
+            grp_t[key] = st("grp", [P, 512, 4], BF16, 6)
+            return grp_t[key]
+
+        def source(key):
+            if key[0] == "al":
+                return raw[key][:]
+            if key[0] == "a":
+                return ds_t[key[1:]][:]
+            t = (x_raw if key[0] == "x" else c_raw)[key[1]]
+            return t[:, :, 512 * key[2] : 512 * (key[2] + 1)]
+
+        def interleave(eng, key, lo=0, hi=512):
+            if lo == 0:
+                grp(key)
+            copy = nc.vector.tensor_copy if eng == "v" else nc.scalar.copy
+            copy(
+                out=grp_t[key][:, lo:hi, :].rearrange("p (c i) t -> p c t i", i=4),
+                in_=source(key)[:, :, lo:hi].rearrange("p t (c i) -> p c t i", i=4),
+            )
+
+        def quant(key):
+            kind = key[0]
+            if kind == "g":
+                q, fmt = g_q[key[1]], E5
+            elif kind == "al":
+                q, fmt = al_q[key[1]], E4
+            elif kind == "x":
+                q, fmt = x_q[key[1]][key[2]], E4
+            elif kind == "c":
+                q, fmt = c_q[key[1]][key[2]], E4
+            elif kind == "a":
+                q, fmt = a_q[key[1:]], E5
+            else:
+                q, fmt = b_q[key[1:]], E5
+            nc.vector.quantize_mx(
+                out=q[0][:].bitcast(fmt), scales=q[1][:], in_=grp_t[key][:].rearrange("p n t -> p (n t)")
+            )
+
+        def mx(out, lhs, lcols, lfmt, rhs, rfmt, start, stop):
+            nc.tensor.matmul_mx(
+                out=out,
+                lhsT=lhs[0][:, lcols].bitcast(lfmt),
+                lhsT_scale=lhs[1][:, lcols],
+                rhs=rhs[0][:].bitcast(rfmt),
+                rhs_scale=rhs[1][:],
+                start=start,
+                stop=stop,
+            )
+
+        def cols(j):
+            return slice(128 * j, 128 * (j + 1))
+
+        def g_transpose(g, pair):
+            if pair == 0:
+                grp(("g", g))
+            words = raw[("g", g)][:].rearrange("p j l -> p (j l)").bitcast(F32).rearrange("p (j w) -> p j w", j=4)
+            b = bank("tb", 2)
+            bv = b[:].rearrange("p (a u r) -> p a u r", a=2, u=2)
+            for a in range(2):
+                for u in range(2):
+                    nc.tensor.transpose(bv[:, a, u, :], words[:, 2 * pair + a, u : 256 : 2], ident[:])
+            return bv
+
+        def g_copy(g, pair, bv, copy):
+            dst = grp_t[("g", g)][:].rearrange("p n t -> p (n t)").bitcast(F32)[:, 512 * pair : 512 * (pair + 1)]
+            copy(
+                out=dst.rearrange("p (a r u) -> p a r u", a=2, u=2),
+                in_=bv.rearrange("p a u r -> p a r u"),
+            )
+
+        def dk(u, j):
+            b = bank("dk", 2)
+            mx(b[:], g_q[u[0]], cols(j), E5, al_q[u[1]], E4, True, True)
+            dk_b[(u, j)] = b
+
+        def mult(u, j):
+            g, h = u
+            if j == 0:
+                ds_t[u] = st("ds", [P, 4, 512], F32, 2)
+            nc.vector.scalar_tensor_tensor(
+                out=ds_t[u][:, j, :].rearrange("p (t q) -> p t q", t=4),
+                in0=dk_b[(u, j)][:].rearrange("p (q t) -> p t q", t=4),
+                scalar=1.0,
+                in1=k_t[u][:, j, :].rearrange("p (q t) -> p t q", t=4),
+                op0=MUL,
+                op1=MUL,
+                accum_out=row[:, g, j, h : h + 1],
+            )
+
+        def t_block(u, j):
+            if j == 0:
+                grp(("b",) + u)
+            b = bank("tb", 2)
+            for t in range(4):
+                nc.tensor.transpose(b[:, cols(t)], ds_t[u][:, j, cols(t)], ident[:])
+            nc.scalar.copy(
+                out=grp_t[("b",) + u][:, cols(j), :],
+                in_=b[:].rearrange("q (t i) -> q i t", t=4),
+            )
+
+        def col_block(u, t):
+            if t == 0:
+                col_b[u] = bank("col", 1)
+            for j in range(4):
+                nc.tensor.matmul(
+                    col_b[u][:, cols(t)], lhsT=ds_t[u][:, j, cols(t)], rhs=ident[:],
+                    is_transpose=True, start=(j == 0), stop=(j == 3),
+                )
+
+        def colred(u):
+            g, h = u
+            nc.vector.tensor_reduce(
+                out=colp[:, g, h, :], in_=col_b[u][:].rearrange("q (t i) -> q t i", t=4), axis=AX, op=ADD
+            )
+
+        def finish_col(h):
+            nc.vector.scalar_tensor_tensor(
+                out=ncol[:, h, :], in0=colp[:, 0, h, :], scalar=-1.0, in1=colp[:, 1, h, :], op0=MUL, op1=SUB
+            )
+
+        def finish_row(g):
+            nc.vector.tensor_reduce(out=nrow[:, g, :], in_=row[:, g, :, :], axis=AX, op=ADD)
+            nc.vector.tensor_scalar(out=nrow[:, g, :], in0=nrow[:, g, :], scalar1=-1.0, scalar2=None, op0=MUL)
+
+        def mm(job, tag="mm", bufs=3, lo=0, hi=None):
+            kind, i, j, f = job
+            if lo == 0:
+                mm_b[job] = bank(tag, bufs)
+            out = mm_b[job][:]
+            if kind == "dc":
+                for g in range(NG):
+                    mx(out, a_q[(g, i)], cols(j), E5, x_q[g][f], E4, g == 0, g == NG - 1)
+            else:
+                for h in range(lo, NH if hi is None else hi):
+                    mx(out, b_q[(i, h)], cols(j), E5, c_q[h][f], E4, h == 0, h == NH - 1)
+
+        def epi(job):
+            kind, i, j, f = job
+            if f == 0:
+                out_t[(kind, i, j)] = st("out", [P, F], F32, 5)
+            o = out_t[(kind, i, j)]
+            fs = slice(512 * f, 512 * (f + 1))
+            src = (c_raw if kind == "dc" else x_raw)[i]
+            fac = (ncol if kind == "dc" else nrow)[:, i, j : j + 1]
+            nc.vector.scalar_tensor_tensor(
+                out=o[:, fs], in0=src[:, j, fs], scalar=fac, in1=mm_b[job][:], op0=MUL, op1=ADD
+            )
+            if f == 1:
+                nc.sync.dma_start(out=(dc_v if kind == "dc" else dx_v)[i, j], in_=o[:])
+
+        def jobs(kind, i):
+            return [(kind, i, j, f) for j in range(4) for f in range(2)]
+
+        load_g(0)
+        load_al(0)
+        load_k(UNITS[0], 2)
+        load_g(1)
+        load_k(UNITS[1])
+        load_al(1)
+        load_x(0)
+        load_x(1)
+        load_k(UNITS[2])
+        load_c(0)
+        load_al(2)
+        later_loads = {0: [("c", 1), ("al", 3)], 1: [("c", 2)], 2: [("c", 3)]}
+
+        b0 = g_transpose(0, 0)
+        b1 = g_transpose(0, 1)
+        g_copy(0, 0, b0, nc.scalar.copy)
+        g_copy(0, 1, b1, nc.vector.tensor_copy)
+        interleave("v", ("al", 0), 0, 256)
+        interleave("s", ("al", 0), 256, 512)
+        quant(("g", 0))
+        quant(("al", 0))
+        u0 = UNITS[0]
+        dk(u0, 0)
+        dk(u0, 1)
+        mult(u0, 0)
+        mult(u0, 1)
+        b0 = g_transpose(1, 0)
+        b1 = g_transpose(1, 1)
+        g_copy(1, 0, b0, nc.scalar.copy)
+        g_copy(1, 1, b1, nc.scalar.copy)
+        dk(u0, 2)
+        dk(u0, 3)
+        mult(u0, 2)
+        mult(u0, 3)
+        quant(("g", 1))
+        load_k(UNITS[3])
+
+        work_v = {0: [("al", 1)], 1: [("x", 1, 1)], 2: [("al", 2)], 3: [("al", 3)]}
+        work_s = {
+            0: [("x", 0, 0), ("x", 0, 1)],
+            1: [("x", 1, 0)],
+            2: [("c", 0, 0), ("c", 0, 1)],
+            3: [("c", 1, 0), ("c", 1, 1)],
+            4: [("c", 2, 0), ("c", 2, 1)],
+            5: [("c", 3, 0), ("c", 3, 1)],
+        }
+        dc = [jobs("dc", h) for h in range(NH)]
+        dx = [jobs("dx", g) for g in range(NG)]
+        mms = {2: dc[0][:4], 3: dc[0][4:], 4: dc[1][:4], 5: dc[1][4:], 6: dx[0], 7: dc[2]}
+
+        for s, u in enumerate(UNITS):
+            nxt = UNITS[s + 1] if s + 1 < len(UNITS) else None
+            for kind, i in later_loads.get(s, []):
+                (load_c if kind == "c" else load_al)(i)
+            todo = mms.get(s, [])
+            half = len(todo) // 2
+
+            for key in work_v.get(s, []):
+                interleave("v", key)
+            for key in work_s.get(s - 1, []):
+                quant(key)
+            if nxt:
+                dk(nxt, 0)
+                dk(nxt, 1)
+            t_block(u, 0)
+            t_block(u, 1)
+            col_block(u, 0)
+            t_block(u, 2)
+            col_block(u, 1)
+            t_block(u, 3)
+            col_block(u, 2)
+            col_block(u, 3)
+            interleave("s", ("a",) + u)
+            for key in work_s.get(s, []):
+                interleave("s", key)
+
+            if nxt:
+                mult(nxt, 0)
+                mult(nxt, 1)
+            colred(u)
+            for key in work_v.get(s, []):
+                quant(key)
+            if (1 - u[0], u[1]) in UNITS[:s]:
+                finish_col(u[1])
+            if s == 5:
+                finish_row(0)
+            if s == 7:
+                finish_row(1)
+            for job in todo[:half]:
+                mm(job)
+                epi(job)
+            quant(("b",) + u)
+            if nxt:
+                dk(nxt, 2)
+                dk(nxt, 3)
+                mult(nxt, 2)
+                mult(nxt, 3)
+                if s + 4 < len(UNITS):
+                    load_k(UNITS[s + 4])
+            quant(("a",) + u)
+            for job in todo[half:]:
+                mm(job)
+                epi(job)
+
+        early = dx[1][:4]
+        for i, job in enumerate(early):
+            mm(job, *(("dk", 2) if i < 2 else ("tb", 2)), 0, NH - 1)
+        for job in early:
+            mm(job, lo=NH - 1)
+            epi(job)
+        for job in dx[1][4:] + dc[3]:
+            mm(job)
+            epi(job)

@@ -10,29 +10,115 @@ F32 = mybir.dt.float32
 BF16 = mybir.dt.bfloat16
 U32 = mybir.dt.uint32
 U8 = mybir.dt.uint8
-E4 = mybir.dt.float8_e4m3fn_x4
-E5 = mybir.dt.float8_e5m2_x4
-MUL = mybir.AluOpType.mult
+E4M3 = mybir.dt.float8_e4m3fn_x4
+E5M2 = mybir.dt.float8_e5m2_x4
+MULT = mybir.AluOpType.mult
 ADD = mybir.AluOpType.add
-SUB = mybir.AluOpType.subtract
-AX = mybir.AxisListType.X
+SUBTRACT = mybir.AluOpType.subtract
+AXIS_X = mybir.AxisListType.X
 
 P = 128
-NG = B // 512
-NH = N // 512
+GROUPS = B // 512
+CHUNKS = N // 512
 
-UNITS = [(0, 0), (1, 0), (0, 1), (1, 1), (0, 2), (0, 3), (1, 2), (1, 3)]
+UNITS = ((0, 0), (1, 0), (0, 1), (1, 1), (0, 2), (0, 3), (1, 2), (1, 3))
+
+SLOTS = dict(mm=4, tb=3, col=1, k=3, raw=3, ds=2, grp=4, out=9)
+ROW_CODES = 8
+OTHER_CODES = 9
+
+PARTS = 2
+
+HOP = 8
+DMA_HOP = 100
+TURN = 15
+TURN_RANKS = 41
+START_G = 35
+
+
+def plan(tasks, slots):
+    room = dict(slots)
+    held = set()
+    users = {}
+    missing = {}
+    ready = {}
+    for name in tasks:
+        missing[name] = len(tasks[name]["needs"])
+        for other in tasks[name]["needs"]:
+            users.setdefault(other, []).append(name)
+        if missing[name] == 0:
+            ready[name] = 0
+    position = {name: i for i, name in enumerate(sorted(tasks, key=lambda n: tasks[n]["rank"]))}
+    waiting = sorted(ready, key=lambda n: position[n])
+    free = {"T": 0, "V": 0, "S": 0, "G": START_G, "Q": 0, "N": 0}
+    port_free = 0
+    port_user = None
+    mode = None
+    now = 0
+    running = []
+    releases = []
+    order = []
+    while waiting or running:
+        started = None
+        fits = [n for n in waiting if ready[n] <= now and (tasks[n]["slot"] is None or tasks[n]["slot"] in held or room[tasks[n]["slot"][0]] > 0)]
+        g_waits = free["G"] <= now and any(e == "G" for n in fits for e, length in tasks[n]["engines"])
+        same_mode = [tasks[n]["rank"] for n in fits if tasks[n]["mode"] == mode]
+        for name in fits:
+            task = tasks[name]
+            turn = task["mode"] is not None and mode is not None and task["mode"] != mode
+            if turn and same_mode and min(same_mode) < task["rank"] + TURN_RANKS:
+                continue
+            for engine, length in task["engines"]:
+                port = engine == "G" or (engine == "V" and task["port"])
+                if free[engine] > now or (port and port_free > now):
+                    continue
+                if port and engine == "V" and port_user == "V" and g_waits:
+                    continue
+                if engine == "T":
+                    mode = task["mode"]
+                    length = length + TURN * turn
+                if task["slot"] and task["slot"] not in held:
+                    held.add(task["slot"])
+                    room[task["slot"][0]] = room[task["slot"][0]] - 1
+                free[engine] = now + length
+                if port:
+                    port_free = now + length
+                    port_user = engine
+                running.append((now + length + (DMA_HOP if engine == "Q" else 0), name, engine))
+                order.append((name, engine))
+                started = name
+                break
+            if started:
+                break
+        if started:
+            waiting.remove(started)
+            continue
+        times = [r[0] for r in running + releases] + [ready[n] for n in waiting] + list(free.values()) + [port_free]
+        now = min(t for t in times if t > now)
+        for r in [r for r in releases if r[0] <= now]:
+            releases.remove(r)
+            room[r[1]] = room[r[1]] + 1
+        for r in sorted([r for r in running if r[0] <= now], key=lambda r: r[0]):
+            running.remove(r)
+            releases.extend([(now + HOP, pool) for pool in tasks[r[1]]["frees"]])
+            for user in users.get(r[1], []):
+                missing[user] = missing[user] - 1
+                direct = r[2] in ("N", "Q") or (r[2] == "T" and tasks[user]["engines"][0][0] == "T")
+                ready[user] = max(ready.get(user, 0), now + (0 if direct else HOP))
+                if missing[user] == 0:
+                    waiting = sorted(waiting + [user], key=lambda n: position[n])
+    return order
 
 
 def tile_autoencoder_pa_v_kernel(tc, x, centers, alpha, k_enc, grad_out, out_0, out_1):
     nc = tc.nc
-    x_v = x.rearrange("(g p j) f -> g p j f", g=NG, j=4)
-    c_v = centers.rearrange("(h p j) f -> h p j f", h=NH, j=4)
-    al_v = alpha.rearrange("(p j) n -> p j n", j=4)
-    k_v = k_enc.rearrange("(g p j) n -> g p j n", g=NG, j=4)
-    g_v = grad_out.rearrange("(g p j) l -> g p j l", g=NG, j=4)
-    dx_v = out_0.rearrange("(g p j) f -> g j p f", g=NG, j=4)
-    dc_v = out_1.rearrange("(h p j) f -> h j p f", h=NH, j=4)
+    x_v = x.rearrange("(g p j) f -> g p j f", g=GROUPS, j=4)
+    c_v = centers.rearrange("(h p t) f -> h p t f", h=CHUNKS, t=4)
+    al_v = alpha.rearrange("(p t) n -> p t n", t=4)
+    k_v = k_enc.rearrange("(g p j) n -> g p j n", g=GROUPS, j=4)
+    g_v = grad_out.rearrange("(g p j) l -> g p j l", g=GROUPS, j=4)
+    dx_v = out_0.rearrange("(g p j) f -> g j p f", g=GROUPS, j=4)
+    dc_v = out_1.rearrange("(h p t) f -> h t p f", h=CHUNKS, t=4)
 
     with ExitStack() as ctx:
         keep = ctx.enter_context(tc.tile_pool(name="keep", bufs=1))
@@ -40,328 +126,287 @@ def tile_autoencoder_pa_v_kernel(tc, x, centers, alpha, k_enc, grad_out, out_0, 
         psum = ctx.enter_context(tc.psum_pool(name="psum", bufs=2))
         ctx.enter_context(tc.manual_schedule())
 
-        def sb(name, shape, dtype):
+        def kept(name, shape, dtype):
             return keep.tile(shape, dtype, name=name, align_bytes=64)
 
-        def st(tag, shape, dtype, bufs):
+        def streamed(tag, shape, dtype, bufs):
             return stream.tile(shape, dtype, name=tag, tag=tag, bufs=bufs, align_bytes=64)
 
-        def bank(tag, bufs):
-            return psum.tile([P, 512], F32, name=tag, tag=tag, bufs=bufs)
+        def bank(tag):
+            return psum.tile([P, 512], F32, name=tag, tag=tag, bufs=SLOTS[tag])
 
-        ident = sb("ident", [P, P], F32)
+        ident = kept("ident", [P, P], F32)
         make_identity(nc, ident[:])
+        x_raw = [kept(f"x_raw{g}", [P, 4, F], BF16) for g in range(GROUPS)]
+        c_raw = [kept(f"c_raw{h}", [P, 4, F], BF16) for h in range(CHUNKS)]
+        row_parts = kept("row_parts", [P, GROUPS, 4, CHUNKS], F32)
+        col_parts = kept("col_parts", [P, GROUPS, CHUNKS, 4], F32)
+        minus_row = kept("minus_row", [P, GROUPS, 4], F32)
+        minus_col = kept("minus_col", [P, CHUNKS, 4], F32)
 
-        x_raw = [sb(f"x_raw{g}", [P, 4, F], BF16) for g in range(NG)]
-        c_raw = [sb(f"c_raw{h}", [P, 4, F], BF16) for h in range(NH)]
-        x_q = [[(sb(f"xc{g}{f}", [P, 512], U32), sb(f"xs{g}{f}", [P, 512], U8)) for f in range(2)] for g in range(NG)]
-        c_q = [[(sb(f"cc{h}{f}", [P, 512], U32), sb(f"cs{h}{f}", [P, 512], U8)) for f in range(2)] for h in range(NH)]
-        al_q = [(sb(f"alc{h}", [P, 512], U32), sb(f"als{h}", [P, 512], U8)) for h in range(NH)]
-        g_q = [(sb(f"gc{g}", [P, 512], U32), sb(f"gs{g}", [P, 512], U8)) for g in range(NG)]
-        a_q = {u: (sb(f"ac{u[0]}{u[1]}", [P, 512], U32), sb(f"as{u[0]}{u[1]}", [P, 512], U8)) for u in UNITS}
-        b_q = {u: (sb(f"bc{u[0]}{u[1]}", [P, 512], U32), sb(f"bs{u[0]}{u[1]}", [P, 512], U8)) for u in UNITS}
-        row = sb("row", [P, NG, 4, NH], F32)
-        nrow = sb("nrow", [P, NG, 4], F32)
-        colp = sb("colp", [P, NG, NH, 4], F32)
-        ncol = sb("ncol", [P, NH, 4], F32)
+        tiles = {}
+        tasks = {}
 
-        raw = {}
-        k_t = {}
-        ds_t = {}
-        grp_t = {}
-        dk_b = {}
-        col_b = {}
-        mm_b = {}
-        out_t = {}
+        def task(name, engines, emit, needs=(), slot=None, frees=(), rank=0, port=False, mode=None):
+            tasks[name] = dict(engines=engines, emit=emit, needs=needs, slot=slot, frees=frees, rank=rank, port=port, mode=mode)
 
-        def load_g(g):
-            t = st("araw", [P, 4, 512], BF16, 3)
-            nc.sync.dma_start(out=t[:], in_=g_v[g])
-            raw[("g", g)] = t
+        def shared(key, make):
+            if key not in tiles:
+                tiles[key] = make()
+            return tiles[key]
 
-        def load_al(h):
-            t = st("araw", [P, 4, 512], BF16, 3)
-            nc.sync.dma_start(out=t[:], in_=al_v[:, :, 512 * h : 512 * (h + 1)])
-            raw[("al", h)] = t
+        def cols(j):
+            return slice(128 * j, 128 * (j + 1))
 
-        def load_k(u, parts=1):
+        place = {u: i for i, u in enumerate(UNITS)}
+        first = {h: min(place[(g, h)] for g in range(GROUPS)) for h in range(CHUNKS)}
+        first_g1 = min(place[(1, h)] for h in range(CHUNKS))
+
+
+        def load(name, length, rank, dst, src, slot=None):
+            task(name, [("Q", length)], lambda engine: nc.sync.dma_start(out=dst(), in_=src), slot=slot, rank=rank)
+
+        def raw(kind, i):
+            return shared(("raw", kind, i), lambda: streamed("raw", [P, 4, 512], BF16, SLOTS["raw"]))
+
+        def k_tile(u):
+            return shared(("k", u), lambda: streamed("k", [P, 4, 512], F32, SLOTS["k"]))
+
+        for h in range(CHUNKS):
+            load(("ld", "al", h), 44, -1000 if h == 0 else 10 * first[h] - 279, lambda h=h: raw("al", h)[:], al_v[:, :, 512 * h : 512 * (h + 1)], ("raw", ("al", h)))
+            load(("ld", "c", h), 87, 325 + 27 * h, lambda h=h: c_raw[h][:], c_v[h])
+        for g in range(GROUPS):
+            load(("ld", "x", g), 87, 620 + g, lambda g=g: x_raw[g][:], x_v[g])
+            for pair in range(2):
+                js = slice(2 * pair, 2 * pair + 2)
+                load(("ld", "g", g, pair), 22, -999 if g == 0 else 10 * first_g1 - 320, lambda g=g, js=js: raw("g", g)[:, js, :], g_v[g, :, js, :], ("raw", ("g", g)))
+        for u in UNITS:
             g, h = u
-            t = st("k", [P, 4, 512], F32, 3)
-            w = 4 // parts
-            for i in range(parts):
-                nc.sync.dma_start(out=t[:, w * i : w * (i + 1), :], in_=k_v[g, :, w * i : w * (i + 1), 512 * h : 512 * (h + 1)])
-            k_t[u] = t
+            for pair in range(2):
+                js = slice(2 * pair, 2 * pair + 2)
+                load(("ld", "k", u, pair), 44, 10 * place[u] - 97, lambda u=u, js=js: k_tile(u)[:, js, :], k_v[g, :, js, 512 * h : 512 * (h + 1)], ("k", u))
 
-        def load_x(g):
-            nc.sync.dma_start(out=x_raw[g][:], in_=x_v[g])
+        def codes(key):
+            def make():
+                if key[0] == "a":
+                    return streamed("a_codes", [P, 512], U32, ROW_CODES), streamed("a_scales", [P, 512], U8, ROW_CODES)
+                if key[0] in ("al", "b"):
+                    return streamed("ab_codes", [P, 512], U32, OTHER_CODES), streamed("ab_scales", [P, 512], U8, OTHER_CODES)
+                name = "_".join(str(k) for k in key)
+                return kept("codes_" + name, [P, 512], U32), kept("scales_" + name, [P, 512], U8)
 
-        def load_c(h):
-            nc.sync.dma_start(out=c_raw[h][:], in_=c_v[h])
+            return shared(("codes",) + key, make)
 
-        def grp(key):
-            grp_t[key] = st("grp", [P, 512, 4], BF16, 6)
-            return grp_t[key]
+        def grouped(key):
+            return shared(("grp",) + key, lambda: streamed("grp", [P, 512, 4], BF16, SLOTS["grp"]))
 
-        def source(key):
-            if key[0] == "al":
-                return raw[key][:]
-            if key[0] == "a":
-                return ds_t[key[1:]][:]
-            t = (x_raw if key[0] == "x" else c_raw)[key[1]]
-            return t[:, :, 512 * key[2] : 512 * (key[2] + 1)]
+        def quantise(key, fmt, n0=0, n1=512):
+            def emit(engine):
+                out, scales = codes(key)
+                nc.vector.quantize_mx(
+                    out=out[:, n0:n1].bitcast(fmt), scales=scales[:, n0:n1], in_=grouped(key)[:, n0:n1, :].rearrange("p n t -> p (n t)")
+                )
 
-        def interleave(eng, key, lo=0, hi=512):
-            if lo == 0:
-                grp(key)
-            copy = nc.vector.tensor_copy if eng == "v" else nc.scalar.copy
-            copy(
-                out=grp_t[key][:, lo:hi, :].rearrange("p (c i) t -> p c t i", i=4),
-                in_=source(key)[:, :, lo:hi].rearrange("p t (c i) -> p c t i", i=4),
-            )
+            return emit
 
-        def quant(key):
-            kind = key[0]
-            if kind == "g":
-                q, fmt = g_q[key[1]], E5
-            elif kind == "al":
-                q, fmt = al_q[key[1]], E4
-            elif kind == "x":
-                q, fmt = x_q[key[1]][key[2]], E4
-            elif kind == "c":
-                q, fmt = c_q[key[1]][key[2]], E4
-            elif kind == "a":
-                q, fmt = a_q[key[1:]], E5
-            else:
-                q, fmt = b_q[key[1:]], E5
-            nc.vector.quantize_mx(
-                out=q[0][:].bitcast(fmt), scales=q[1][:], in_=grp_t[key][:].rearrange("p n t -> p (n t)")
-            )
+        def interleave(key, source, i):
+            def emit(engine):
+                part = slice(512 // PARTS * i, 512 // PARTS * (i + 1))
+                out = grouped(key)[:, part, :].rearrange("p (c n) t -> p c t n", n=4)
+                in_ = source()[:, :, part].rearrange("p t (c n) -> p c t n", n=4)
+                if engine == "V":
+                    nc.vector.tensor_copy(out=out, in_=in_)
+                elif engine == "S":
+                    nc.scalar.copy(out=out, in_=in_)
+                else:
+                    for c in range(0, 128 // PARTS, 16):
+                        piece = slice(c, c + 16)
+                        nc.gpsimd.tensor_scalar(out=out[:, piece], in0=in_[:, piece], scalar1=1.0, scalar2=0.0, op0=MULT, op1=ADD)
 
-        def mx(out, lhs, lcols, lfmt, rhs, rfmt, start, stop):
+            return emit
+
+        def operand(key, source, fmt, needs, rank, engines, frees=()):
+            for i in range(PARTS):
+                task(("i",) + key + (i,), engines, interleave(key, source, i), needs, ("grp", key), rank=rank, port=True)
+            task(("q",) + key, [("V", 24)], quantise(key, fmt), [("i",) + key + (i,) for i in range(PARTS)], frees=["grp"] + list(frees), rank=rank, port=True)
+
+        for h in range(CHUNKS):
+            operand(("al", h), lambda h=h: raw("al", h), E4M3, [("ld", "al", h)], -1000 if h == 0 else 10 * first[h] - 182, [("V", 24), ("S", 44)], ["raw"])
+        for f in range(2):
+            half = slice(512 * f, 512 * (f + 1))
+            for g in range(GROUPS):
+                operand(("x", g, f), lambda g=g, half=half: x_raw[g][:, :, half], E4M3, [("ld", "x", g)], 43 + 1082 * f + g, [("S", 44)])
+            for h in range(CHUNKS):
+                operand(("c", h, f), lambda h=h, half=half: c_raw[h][:, :, half], E4M3, [("ld", "c", h)], 326 + 284 * f + 27 * h, [("S", 44)])
+
+        def g_transpose(g, pair):
+            def emit(engine):
+                words = raw("g", g)[:].rearrange("p j l -> p (j l)").bitcast(F32).rearrange("p (j w) -> p j w", j=4)
+                tiles[("gt", g, pair)] = bank("tb")
+                b = tiles[("gt", g, pair)][:].rearrange("q (j u p) -> q j u p", j=2, u=2)
+                for j in range(2):
+                    for u in range(2):
+                        nc.tensor.transpose(b[:, j, u, :], words[:, 2 * pair + j, u:256:2], ident[:])
+
+            return emit
+
+        def g_copy(g, pair):
+            def emit(engine):
+                out = grouped(("g", g))[:].rearrange("q n t -> q (n t)").bitcast(F32)[:, 512 * pair : 512 * (pair + 1)]
+                copy = nc.scalar.copy if engine == "S" else nc.vector.tensor_copy
+                copy(
+                    out=out.rearrange("q (j p u) -> q j p u", j=2, u=2),
+                    in_=tiles[("gt", g, pair)][:].rearrange("q (j u p) -> q j p u", j=2, u=2),
+                )
+
+            return emit
+
+        for g in range(GROUPS):
+            rank = -999 if g == 0 else 10 * first_g1 - 20
+            for pair in range(2):
+                task(("gt", g, pair), [("T", 21)], g_transpose(g, pair), [("ld", "g", g, pair)], ("tb", ("g", g, pair)), rank=rank, mode="transpose")
+                task(("gc", g, pair), [("S", 22), ("V", 22)], g_copy(g, pair), [("gt", g, pair)], ("grp", ("g", g)), ["tb"], rank)
+                task(("q", "g", g, pair), [("V", 12)], quantise(("g", g), E5M2, 256 * pair, 256 * (pair + 1)), [("gc", g, pair)], rank=rank, port=True)
+            task(("free", "g", g), [("N", 0)], lambda engine: None, [("q", "g", g, pair) for pair in range(2)], frees=["raw", "grp"])
+
+        def mx(out, lhs, lhs_cols, lhs_fmt, rhs, rhs_fmt, start, stop):
             nc.tensor.matmul_mx(
-                out=out,
-                lhsT=lhs[0][:, lcols].bitcast(lfmt),
-                lhsT_scale=lhs[1][:, lcols],
-                rhs=rhs[0][:].bitcast(rfmt),
+                out=out[:],
+                lhsT=lhs[0][:, lhs_cols].bitcast(lhs_fmt),
+                lhsT_scale=lhs[1][:, lhs_cols],
+                rhs=rhs[0][:].bitcast(rhs_fmt),
                 rhs_scale=rhs[1][:],
                 start=start,
                 stop=stop,
             )
 
-        def cols(j):
-            return slice(128 * j, 128 * (j + 1))
-
-        def g_transpose(g, pair):
-            if pair == 0:
-                grp(("g", g))
-            words = raw[("g", g)][:].rearrange("p j l -> p (j l)").bitcast(F32).rearrange("p (j w) -> p j w", j=4)
-            b = bank("tb", 2)
-            bv = b[:].rearrange("p (a u r) -> p a u r", a=2, u=2)
-            for a in range(2):
-                for u in range(2):
-                    nc.tensor.transpose(bv[:, a, u, :], words[:, 2 * pair + a, u : 256 : 2], ident[:])
-            return bv
-
-        def g_copy(g, pair, bv, copy):
-            dst = grp_t[("g", g)][:].rearrange("p n t -> p (n t)").bitcast(F32)[:, 512 * pair : 512 * (pair + 1)]
-            copy(
-                out=dst.rearrange("p (a r u) -> p a r u", a=2, u=2),
-                in_=bv.rearrange("p a u r -> p a r u"),
-            )
+        def ds_tile(u):
+            return shared(("ds", u), lambda: streamed("ds", [P, 4, 512], F32, SLOTS["ds"]))
 
         def dk(u, j):
-            b = bank("dk", 2)
-            mx(b[:], g_q[u[0]], cols(j), E5, al_q[u[1]], E4, True, True)
-            dk_b[(u, j)] = b
+            def emit(engine):
+                tiles[("dk", u, j)] = bank("mm")
+                mx(tiles[("dk", u, j)], codes(("g", u[0])), cols(j), E5M2, codes(("al", u[1])), E4M3, True, True)
 
-        def mult(u, j):
-            g, h = u
-            if j == 0:
-                ds_t[u] = st("ds", [P, 4, 512], F32, 2)
-            nc.vector.scalar_tensor_tensor(
-                out=ds_t[u][:, j, :].rearrange("p (t q) -> p t q", t=4),
-                in0=dk_b[(u, j)][:].rearrange("p (q t) -> p t q", t=4),
-                scalar=1.0,
-                in1=k_t[u][:, j, :].rearrange("p (q t) -> p t q", t=4),
-                op0=MUL,
-                op1=MUL,
-                accum_out=row[:, g, j, h : h + 1],
-            )
+            return emit
 
-        def t_block(u, j):
-            if j == 0:
-                grp(("b",) + u)
-            b = bank("tb", 2)
-            for t in range(4):
-                nc.tensor.transpose(b[:, cols(t)], ds_t[u][:, j, cols(t)], ident[:])
-            nc.scalar.copy(
-                out=grp_t[("b",) + u][:, cols(j), :],
-                in_=b[:].rearrange("q (t i) -> q i t", t=4),
-            )
-
-        def col_block(u, t):
-            if t == 0:
-                col_b[u] = bank("col", 1)
-            for j in range(4):
-                nc.tensor.matmul(
-                    col_b[u][:, cols(t)], lhsT=ds_t[u][:, j, cols(t)], rhs=ident[:],
-                    is_transpose=True, start=(j == 0), stop=(j == 3),
+        def product(u, j):
+            def emit(engine):
+                nc.vector.scalar_tensor_tensor(
+                    out=ds_tile(u)[:, j, :].rearrange("p (t q) -> p q t", t=4),
+                    in0=tiles[("dk", u, j)][:].rearrange("p (q t) -> p q t", t=4),
+                    scalar=1.0,
+                    in1=k_tile(u)[:, j, :].rearrange("p (q t) -> p q t", t=4),
+                    op0=MULT,
+                    op1=MULT,
+                    accum_out=row_parts[:, u[0], j, u[1] : u[1] + 1],
                 )
 
-        def colred(u):
+            return emit
+
+        def transpose(u, j):
+            def emit(engine):
+                tiles[("dsT", u, j)] = bank("tb")
+                for t in range(4):
+                    nc.tensor.transpose(tiles[("dsT", u, j)][:, cols(t)], ds_tile(u)[:, j, cols(t)], ident[:])
+
+            return emit
+
+        def transposed_copy(u, j):
+            def emit(engine):
+                nc.scalar.copy(out=grouped(("b",) + u)[:, cols(j), :], in_=tiles[("dsT", u, j)][:].rearrange("q (t p) -> q p t", t=4))
+
+            return emit
+
+        def add_up(u, t):
+            def emit(engine):
+                b = shared(("col", u), lambda: bank("col"))
+                for j in range(4):
+                    nc.tensor.matmul(b[:, cols(t)], lhsT=ds_tile(u)[:, j, cols(t)], rhs=ident[:], is_transpose=True, start=(j == 0), stop=(j == 3))
+
+            return emit
+
+        def column_sums(u):
+            def emit(engine):
+                nc.vector.tensor_reduce(out=col_parts[:, u[0], u[1], :], in_=tiles[("col", u)][:].rearrange("q (t p) -> q t p", t=4), axis=AXIS_X, op=ADD)
+
+            return emit
+
+        for i, u in enumerate(UNITS):
             g, h = u
-            nc.vector.tensor_reduce(
-                out=colp[:, g, h, :], in_=col_b[u][:].rearrange("q (t i) -> q t i", t=4), axis=AX, op=ADD
-            )
+            products = [("product", u, j) for j in range(4)]
+            for j in range(4):
+                task(("dk", u, j), [("T", 11)], dk(u, j), [("q", "g", g, j // 2), ("q", "al", h)], ("mm", ("dk", u, j)), rank=10 * i + 97, mode="mx")
+                task(("product", u, j), [("V", 29)], product(u, j), [("dk", u, j), ("ld", "k", u, j // 2)], ("ds", u), ["mm", "k"] if j == 3 else ["mm"], 10 * i + 453)
+                task(("dsT", u, j), [("T", 13)], transpose(u, j), [("product", u, j)], ("tb", (u, j)), rank=10 * i, mode="transpose")
+                task(("copy", u, j), [("S", 23)], transposed_copy(u, j), [("dsT", u, j)], ("grp", ("b",) + u), ["tb"], 10 * i)
+                task(("add", u, j), [("T", 13)], add_up(u, j), products, ("col", u), rank=10 * i - 257, mode="transpose")
+            task(("q", "b") + u, [("V", 24)], quantise(("b",) + u, E5M2), [("copy", u, j) for j in range(4)], frees=["grp"], rank=10 * i - 650, port=True)
+            task(("col", u), [("V", 23)], column_sums(u), [("add", u, t) for t in range(4)], frees=["col"], rank=10 * i + 366)
+            operand(("a",) + u, lambda u=u: ds_tile(u), E5M2, products, 10 * i - 49, [("S", 46), ("G", 66)])
+            readers = [("dsT", u, j) for j in range(4)] + [("add", u, t) for t in range(4)] + [("i", "a") + u + (n,) for n in range(PARTS)]
+            task(("free", "ds", u), [("N", 0)], lambda engine: None, readers, frees=["ds"])
 
-        def finish_col(h):
-            nc.vector.scalar_tensor_tensor(
-                out=ncol[:, h, :], in0=colp[:, 0, h, :], scalar=-1.0, in1=colp[:, 1, h, :], op0=MUL, op1=SUB
-            )
+        def multiply(key):
+            kind, i, j, f = key
 
-        def finish_row(g):
-            nc.vector.tensor_reduce(out=nrow[:, g, :], in_=row[:, g, :, :], axis=AX, op=ADD)
-            nc.vector.tensor_scalar(out=nrow[:, g, :], in0=nrow[:, g, :], scalar1=-1.0, scalar2=None, op0=MUL)
+            def emit(engine):
+                tiles[key] = bank("mm")
+                if kind == "dc":
+                    for g in range(GROUPS):
+                        mx(tiles[key], codes(("a", g, i)), cols(j), E5M2, codes(("x", g, f)), E4M3, g == 0, g == GROUPS - 1)
+                else:
+                    for h in range(CHUNKS):
+                        mx(tiles[key], codes(("b", i, h)), cols(j), E5M2, codes(("c", h, f)), E4M3, h == 0, h == CHUNKS - 1)
 
-        def mm(job, tag="mm", bufs=3, lo=0, hi=None):
-            kind, i, j, f = job
-            if lo == 0:
-                mm_b[job] = bank(tag, bufs)
-            out = mm_b[job][:]
-            if kind == "dc":
-                for g in range(NG):
-                    mx(out, a_q[(g, i)], cols(j), E5, x_q[g][f], E4, g == 0, g == NG - 1)
-            else:
-                for h in range(lo, NH if hi is None else hi):
-                    mx(out, b_q[(i, h)], cols(j), E5, c_q[h][f], E4, h == 0, h == NH - 1)
+            return emit
 
-        def epi(job):
-            kind, i, j, f = job
-            if f == 0:
-                out_t[(kind, i, j)] = st("out", [P, F], F32, 5)
-            o = out_t[(kind, i, j)]
-            fs = slice(512 * f, 512 * (f + 1))
-            src = (c_raw if kind == "dc" else x_raw)[i]
-            fac = (ncol if kind == "dc" else nrow)[:, i, j : j + 1]
-            nc.vector.scalar_tensor_tensor(
-                out=o[:, fs], in0=src[:, j, fs], scalar=fac, in1=mm_b[job][:], op0=MUL, op1=ADD
-            )
-            if f == 1:
-                nc.sync.dma_start(out=(dc_v if kind == "dc" else dx_v)[i, j], in_=o[:])
+        def negated_col(h):
+            nc.vector.scalar_tensor_tensor(out=minus_col[:, h, :], in0=col_parts[:, 0, h, :], scalar=-1.0, in1=col_parts[:, 1, h, :], op0=MULT, op1=SUBTRACT)
+            return minus_col[:, h, :]
 
-        def jobs(kind, i):
-            return [(kind, i, j, f) for j in range(4) for f in range(2)]
+        def negated_row(g):
+            nc.vector.tensor_reduce(out=minus_row[:, g, :], in_=row_parts[:, g, :, :], axis=AXIS_X, op=ADD)
+            nc.vector.tensor_scalar(out=minus_row[:, g, :], in0=minus_row[:, g, :], scalar1=-1.0, scalar2=None, op0=MULT)
+            return minus_row[:, g, :]
 
-        load_g(0)
-        load_al(0)
-        load_k(UNITS[0], 2)
-        load_g(1)
-        load_k(UNITS[1])
-        load_al(1)
-        load_x(0)
-        load_x(1)
-        load_k(UNITS[2])
-        load_c(0)
-        load_al(2)
-        later_loads = {0: [("c", 1), ("al", 3)], 1: [("c", 2)], 2: [("c", 3)]}
+        def finish(key):
+            kind, i, j, f = key
 
-        b0 = g_transpose(0, 0)
-        b1 = g_transpose(0, 1)
-        g_copy(0, 0, b0, nc.scalar.copy)
-        g_copy(0, 1, b1, nc.vector.tensor_copy)
-        interleave("v", ("al", 0), 0, 256)
-        interleave("s", ("al", 0), 256, 512)
-        quant(("g", 0))
-        quant(("al", 0))
-        u0 = UNITS[0]
-        dk(u0, 0)
-        dk(u0, 1)
-        mult(u0, 0)
-        mult(u0, 1)
-        b0 = g_transpose(1, 0)
-        b1 = g_transpose(1, 1)
-        g_copy(1, 0, b0, nc.scalar.copy)
-        g_copy(1, 1, b1, nc.scalar.copy)
-        dk(u0, 2)
-        dk(u0, 3)
-        mult(u0, 2)
-        mult(u0, 3)
-        quant(("g", 1))
-        load_k(UNITS[3])
+            def emit(engine):
+                factor = shared(("minus", kind, i), lambda: negated_col(i) if kind == "dc" else negated_row(i))
+                tiles[("out",) + key] = streamed("out", [P, 512], F32, SLOTS["out"])
+                nc.vector.scalar_tensor_tensor(
+                    out=tiles[("out",) + key][:],
+                    in0=(c_raw if kind == "dc" else x_raw)[i][:, j, 512 * f : 512 * (f + 1)],
+                    scalar=factor[:, j : j + 1],
+                    in1=tiles[key][:],
+                    op0=MULT,
+                    op1=ADD,
+                )
 
-        work_v = {0: [("al", 1)], 1: [("x", 1, 1)], 2: [("al", 2)], 3: [("al", 3)]}
-        work_s = {
-            0: [("x", 0, 0), ("x", 0, 1)],
-            1: [("x", 1, 0)],
-            2: [("c", 0, 0), ("c", 0, 1)],
-            3: [("c", 1, 0), ("c", 1, 1)],
-            4: [("c", 2, 0), ("c", 2, 1)],
-            5: [("c", 3, 0), ("c", 3, 1)],
-        }
-        dc = [jobs("dc", h) for h in range(NH)]
-        dx = [jobs("dx", g) for g in range(NG)]
-        mms = {2: dc[0][:4], 3: dc[0][4:], 4: dc[1][:4], 5: dc[1][4:], 6: dx[0], 7: dc[2]}
+            return emit
 
-        for s, u in enumerate(UNITS):
-            nxt = UNITS[s + 1] if s + 1 < len(UNITS) else None
-            for kind, i in later_loads.get(s, []):
-                (load_c if kind == "c" else load_al)(i)
-            todo = mms.get(s, [])
-            half = len(todo) // 2
+        def store(key):
+            kind, i, j, f = key
+            dst = (dc_v if kind == "dc" else dx_v)[i, j, :, 512 * f : 512 * (f + 1)]
+            return lambda engine: nc.sync.dma_start(out=dst, in_=tiles[("out",) + key][:])
 
-            for key in work_v.get(s, []):
-                interleave("v", key)
-            for key in work_s.get(s - 1, []):
-                quant(key)
-            if nxt:
-                dk(nxt, 0)
-                dk(nxt, 1)
-            t_block(u, 0)
-            t_block(u, 1)
-            col_block(u, 0)
-            t_block(u, 2)
-            col_block(u, 1)
-            t_block(u, 3)
-            col_block(u, 2)
-            col_block(u, 3)
-            interleave("s", ("a",) + u)
-            for key in work_s.get(s, []):
-                interleave("s", key)
+        def gradient_tile(key, length, needs, rank, more):
+            task(("mm", key), [("T", length)], multiply(key), needs, ("mm", key), rank=rank, mode="mx")
+            task(("finish", key), [("V", 23)], finish(key), [("mm", key)] + more, ("out", key), ["mm"], rank)
+            task(("store", key), [("Q", 22)], store(key), [("finish", key)], frees=["out"], rank=1000)
 
-            if nxt:
-                mult(nxt, 0)
-                mult(nxt, 1)
-            colred(u)
-            for key in work_v.get(s, []):
-                quant(key)
-            if (1 - u[0], u[1]) in UNITS[:s]:
-                finish_col(u[1])
-            if s == 5:
-                finish_row(0)
-            if s == 7:
-                finish_row(1)
-            for job in todo[:half]:
-                mm(job)
-                epi(job)
-            quant(("b",) + u)
-            if nxt:
-                dk(nxt, 2)
-                dk(nxt, 3)
-                mult(nxt, 2)
-                mult(nxt, 3)
-                if s + 4 < len(UNITS):
-                    load_k(UNITS[s + 4])
-            quant(("a",) + u)
-            for job in todo[half:]:
-                mm(job)
-                epi(job)
+        for f in range(2):
+            for j in range(4):
+                for h in range(CHUNKS):
+                    last = max(place[(g, h)] for g in range(GROUPS))
+                    needs = [("q", "a", g, h) for g in range(GROUPS)] + [("q", "x", g, f) for g in range(GROUPS)]
+                    sums = [("ld", "c", h)] + [("col", (g, h)) for g in range(GROUPS)]
+                    gradient_tile(("dc", h, j, f), 22, needs, -1136 + 200 * last - 482 * f + j, sums)
+                for g in range(GROUPS):
+                    needs = [("q", "b", g, h) for h in range(CHUNKS)] + [("q", "c", h, f) for h in range(CHUNKS)]
+                    gradient_tile(("dx", g, j, f), 44, needs, 38 + 1433 * g - 396 * f + j, [("ld", "x", g)])
 
-        early = dx[1][:4]
-        for i, job in enumerate(early):
-            mm(job, *(("dk", 2) if i < 2 else ("tb", 2)), 0, NH - 1)
-        for job in early:
-            mm(job, lo=NH - 1)
-            epi(job)
-        for job in dx[1][4:] + dc[3]:
-            mm(job)
-            epi(job)
+        for name, engine in plan(tasks, SLOTS):
+            tasks[name]["emit"](engine)

from contextlib import ExitStack

import concourse.mybir as mybir
from concourse.masks import make_identity

B, N, F, L = 1024, 2048, 1024, 512
FLOPS = 2 * B * N * L + 2 * (2 * B * N * F)

F32 = mybir.dt.float32
BF16 = mybir.dt.bfloat16
U32 = mybir.dt.uint32
U8 = mybir.dt.uint8
E4M3 = mybir.dt.float8_e4m3fn_x4
E5M2 = mybir.dt.float8_e5m2_x4
MULT = mybir.AluOpType.mult
ADD = mybir.AluOpType.add
SUBTRACT = mybir.AluOpType.subtract
AXIS_X = mybir.AxisListType.X

P = 128
GROUPS = B // 512
CHUNKS = N // 512

UNITS = ((0, 0), (1, 0), (0, 1), (1, 1), (0, 2), (0, 3), (1, 2), (1, 3))

SLOTS = dict(mm=4, tb=3, col=1, k=3, raw=3, ds=2, grp=4, out=9)
ROW_CODES = 8
OTHER_CODES = 9

PARTS = 2

HOP = 8
DMA_HOP = 100
TURN = 15
TURN_RANKS = 41
START_G = 35


def plan(tasks, slots):
    room = dict(slots)
    held = set()
    users = {}
    missing = {}
    ready = {}
    for name in tasks:
        missing[name] = len(tasks[name]["needs"])
        for other in tasks[name]["needs"]:
            users.setdefault(other, []).append(name)
        if missing[name] == 0:
            ready[name] = 0
    position = {name: i for i, name in enumerate(sorted(tasks, key=lambda n: tasks[n]["rank"]))}
    waiting = sorted(ready, key=lambda n: position[n])
    free = {"T": 0, "V": 0, "S": 0, "G": START_G, "Q": 0, "N": 0}
    port_free = 0
    port_user = None
    mode = None
    now = 0
    running = []
    releases = []
    order = []
    while waiting or running:
        started = None
        fits = [n for n in waiting if ready[n] <= now and (tasks[n]["slot"] is None or tasks[n]["slot"] in held or room[tasks[n]["slot"][0]] > 0)]
        g_waits = free["G"] <= now and any(e == "G" for n in fits for e, length in tasks[n]["engines"])
        same_mode = [tasks[n]["rank"] for n in fits if tasks[n]["mode"] == mode]
        for name in fits:
            task = tasks[name]
            turn = task["mode"] is not None and mode is not None and task["mode"] != mode
            if turn and same_mode and min(same_mode) < task["rank"] + TURN_RANKS:
                continue
            for engine, length in task["engines"]:
                port = engine == "G" or (engine == "V" and task["port"])
                if free[engine] > now or (port and port_free > now):
                    continue
                if port and engine == "V" and port_user == "V" and g_waits:
                    continue
                if engine == "T":
                    mode = task["mode"]
                    length = length + TURN * turn
                if task["slot"] and task["slot"] not in held:
                    held.add(task["slot"])
                    room[task["slot"][0]] = room[task["slot"][0]] - 1
                free[engine] = now + length
                if port:
                    port_free = now + length
                    port_user = engine
                running.append((now + length + (DMA_HOP if engine == "Q" else 0), name, engine))
                order.append((name, engine))
                started = name
                break
            if started:
                break
        if started:
            waiting.remove(started)
            continue
        times = [r[0] for r in running + releases] + [ready[n] for n in waiting] + list(free.values()) + [port_free]
        now = min(t for t in times if t > now)
        for r in [r for r in releases if r[0] <= now]:
            releases.remove(r)
            room[r[1]] = room[r[1]] + 1
        for r in sorted([r for r in running if r[0] <= now], key=lambda r: r[0]):
            running.remove(r)
            releases.extend([(now + HOP, pool) for pool in tasks[r[1]]["frees"]])
            for user in users.get(r[1], []):
                missing[user] = missing[user] - 1
                direct = r[2] in ("N", "Q") or (r[2] == "T" and tasks[user]["engines"][0][0] == "T")
                ready[user] = max(ready.get(user, 0), now + (0 if direct else HOP))
                if missing[user] == 0:
                    waiting = sorted(waiting + [user], key=lambda n: position[n])
    return order


def tile_autoencoder_pa_v_kernel(tc, x, centers, alpha, k_enc, grad_out, out_0, out_1):
    nc = tc.nc
    x_v = x.rearrange("(g p j) f -> g p j f", g=GROUPS, j=4)
    c_v = centers.rearrange("(h p t) f -> h p t f", h=CHUNKS, t=4)
    al_v = alpha.rearrange("(p t) n -> p t n", t=4)
    k_v = k_enc.rearrange("(g p j) n -> g p j n", g=GROUPS, j=4)
    g_v = grad_out.rearrange("(g p j) l -> g p j l", g=GROUPS, j=4)
    dx_v = out_0.rearrange("(g p j) f -> g j p f", g=GROUPS, j=4)
    dc_v = out_1.rearrange("(h p t) f -> h t p f", h=CHUNKS, t=4)

    with ExitStack() as ctx:
        keep = ctx.enter_context(tc.tile_pool(name="keep", bufs=1))
        stream = ctx.enter_context(tc.tile_pool(name="stream", bufs=2))
        psum = ctx.enter_context(tc.psum_pool(name="psum", bufs=2))
        ctx.enter_context(tc.manual_schedule())

        def kept(name, shape, dtype):
            return keep.tile(shape, dtype, name=name, align_bytes=64)

        def streamed(tag, shape, dtype, bufs):
            return stream.tile(shape, dtype, name=tag, tag=tag, bufs=bufs, align_bytes=64)

        def bank(tag):
            return psum.tile([P, 512], F32, name=tag, tag=tag, bufs=SLOTS[tag])

        ident = kept("ident", [P, P], F32)
        make_identity(nc, ident[:])
        x_raw = [kept(f"x_raw{g}", [P, 4, F], BF16) for g in range(GROUPS)]
        c_raw = [kept(f"c_raw{h}", [P, 4, F], BF16) for h in range(CHUNKS)]
        row_parts = kept("row_parts", [P, GROUPS, 4, CHUNKS], F32)
        col_parts = kept("col_parts", [P, GROUPS, CHUNKS, 4], F32)
        minus_row = kept("minus_row", [P, GROUPS, 4], F32)
        minus_col = kept("minus_col", [P, CHUNKS, 4], F32)

        tiles = {}
        tasks = {}

        def task(name, engines, emit, needs=(), slot=None, frees=(), rank=0, port=False, mode=None):
            tasks[name] = dict(engines=engines, emit=emit, needs=needs, slot=slot, frees=frees, rank=rank, port=port, mode=mode)

        def shared(key, make):
            if key not in tiles:
                tiles[key] = make()
            return tiles[key]

        def cols(j):
            return slice(128 * j, 128 * (j + 1))

        place = {u: i for i, u in enumerate(UNITS)}
        first = {h: min(place[(g, h)] for g in range(GROUPS)) for h in range(CHUNKS)}
        first_g1 = min(place[(1, h)] for h in range(CHUNKS))


        def load(name, length, rank, dst, src, slot=None):
            task(name, [("Q", length)], lambda engine: nc.sync.dma_start(out=dst(), in_=src), slot=slot, rank=rank)

        def raw(kind, i):
            return shared(("raw", kind, i), lambda: streamed("raw", [P, 4, 512], BF16, SLOTS["raw"]))

        def k_tile(u):
            return shared(("k", u), lambda: streamed("k", [P, 4, 512], F32, SLOTS["k"]))

        for h in range(CHUNKS):
            load(("ld", "al", h), 44, -1000 if h == 0 else 10 * first[h] - 279, lambda h=h: raw("al", h)[:], al_v[:, :, 512 * h : 512 * (h + 1)], ("raw", ("al", h)))
            load(("ld", "c", h), 87, 325 + 27 * h, lambda h=h: c_raw[h][:], c_v[h])
        for g in range(GROUPS):
            load(("ld", "x", g), 87, 620 + g, lambda g=g: x_raw[g][:], x_v[g])
            for pair in range(2):
                js = slice(2 * pair, 2 * pair + 2)
                load(("ld", "g", g, pair), 22, -999 if g == 0 else 10 * first_g1 - 320, lambda g=g, js=js: raw("g", g)[:, js, :], g_v[g, :, js, :], ("raw", ("g", g)))
        for u in UNITS:
            g, h = u
            for pair in range(2):
                js = slice(2 * pair, 2 * pair + 2)
                load(("ld", "k", u, pair), 44, 10 * place[u] - 97, lambda u=u, js=js: k_tile(u)[:, js, :], k_v[g, :, js, 512 * h : 512 * (h + 1)], ("k", u))

        def codes(key):
            def make():
                if key[0] == "a":
                    return streamed("a_codes", [P, 512], U32, ROW_CODES), streamed("a_scales", [P, 512], U8, ROW_CODES)
                if key[0] in ("al", "b"):
                    return streamed("ab_codes", [P, 512], U32, OTHER_CODES), streamed("ab_scales", [P, 512], U8, OTHER_CODES)
                name = "_".join(str(k) for k in key)
                return kept("codes_" + name, [P, 512], U32), kept("scales_" + name, [P, 512], U8)

            return shared(("codes",) + key, make)

        def grouped(key):
            return shared(("grp",) + key, lambda: streamed("grp", [P, 512, 4], BF16, SLOTS["grp"]))

        def quantise(key, fmt, n0=0, n1=512):
            def emit(engine):
                out, scales = codes(key)
                nc.vector.quantize_mx(
                    out=out[:, n0:n1].bitcast(fmt), scales=scales[:, n0:n1], in_=grouped(key)[:, n0:n1, :].rearrange("p n t -> p (n t)")
                )

            return emit

        def interleave(key, source, i):
            def emit(engine):
                part = slice(512 // PARTS * i, 512 // PARTS * (i + 1))
                out = grouped(key)[:, part, :].rearrange("p (c n) t -> p c t n", n=4)
                in_ = source()[:, :, part].rearrange("p t (c n) -> p c t n", n=4)
                if engine == "V":
                    nc.vector.tensor_copy(out=out, in_=in_)
                elif engine == "S":
                    nc.scalar.copy(out=out, in_=in_)
                else:
                    for c in range(0, 128 // PARTS, 16):
                        piece = slice(c, c + 16)
                        nc.gpsimd.tensor_scalar(out=out[:, piece], in0=in_[:, piece], scalar1=1.0, scalar2=0.0, op0=MULT, op1=ADD)

            return emit

        def operand(key, source, fmt, needs, rank, engines, frees=()):
            for i in range(PARTS):
                task(("i",) + key + (i,), engines, interleave(key, source, i), needs, ("grp", key), rank=rank, port=True)
            task(("q",) + key, [("V", 24)], quantise(key, fmt), [("i",) + key + (i,) for i in range(PARTS)], frees=["grp"] + list(frees), rank=rank, port=True)

        for h in range(CHUNKS):
            operand(("al", h), lambda h=h: raw("al", h), E4M3, [("ld", "al", h)], -1000 if h == 0 else 10 * first[h] - 182, [("V", 24), ("S", 44)], ["raw"])
        for f in range(2):
            half = slice(512 * f, 512 * (f + 1))
            for g in range(GROUPS):
                operand(("x", g, f), lambda g=g, half=half: x_raw[g][:, :, half], E4M3, [("ld", "x", g)], 43 + 1082 * f + g, [("S", 44)])
            for h in range(CHUNKS):
                operand(("c", h, f), lambda h=h, half=half: c_raw[h][:, :, half], E4M3, [("ld", "c", h)], 326 + 284 * f + 27 * h, [("S", 44)])

        def g_transpose(g, pair):
            def emit(engine):
                words = raw("g", g)[:].rearrange("p j l -> p (j l)").bitcast(F32).rearrange("p (j w) -> p j w", j=4)
                tiles[("gt", g, pair)] = bank("tb")
                b = tiles[("gt", g, pair)][:].rearrange("q (j u p) -> q j u p", j=2, u=2)
                for j in range(2):
                    for u in range(2):
                        nc.tensor.transpose(b[:, j, u, :], words[:, 2 * pair + j, u:256:2], ident[:])

            return emit

        def g_copy(g, pair):
            def emit(engine):
                out = grouped(("g", g))[:].rearrange("q n t -> q (n t)").bitcast(F32)[:, 512 * pair : 512 * (pair + 1)]
                copy = nc.scalar.copy if engine == "S" else nc.vector.tensor_copy
                copy(
                    out=out.rearrange("q (j p u) -> q j p u", j=2, u=2),
                    in_=tiles[("gt", g, pair)][:].rearrange("q (j u p) -> q j p u", j=2, u=2),
                )

            return emit

        for g in range(GROUPS):
            rank = -999 if g == 0 else 10 * first_g1 - 20
            for pair in range(2):
                task(("gt", g, pair), [("T", 21)], g_transpose(g, pair), [("ld", "g", g, pair)], ("tb", ("g", g, pair)), rank=rank, mode="transpose")
                task(("gc", g, pair), [("S", 22), ("V", 22)], g_copy(g, pair), [("gt", g, pair)], ("grp", ("g", g)), ["tb"], rank)
                task(("q", "g", g, pair), [("V", 12)], quantise(("g", g), E5M2, 256 * pair, 256 * (pair + 1)), [("gc", g, pair)], rank=rank, port=True)
            task(("free", "g", g), [("N", 0)], lambda engine: None, [("q", "g", g, pair) for pair in range(2)], frees=["raw", "grp"])

        def mx(out, lhs, lhs_cols, lhs_fmt, rhs, rhs_fmt, start, stop):
            nc.tensor.matmul_mx(
                out=out[:],
                lhsT=lhs[0][:, lhs_cols].bitcast(lhs_fmt),
                lhsT_scale=lhs[1][:, lhs_cols],
                rhs=rhs[0][:].bitcast(rhs_fmt),
                rhs_scale=rhs[1][:],
                start=start,
                stop=stop,
            )

        def ds_tile(u):
            return shared(("ds", u), lambda: streamed("ds", [P, 4, 512], F32, SLOTS["ds"]))

        def dk(u, j):
            def emit(engine):
                tiles[("dk", u, j)] = bank("mm")
                mx(tiles[("dk", u, j)], codes(("g", u[0])), cols(j), E5M2, codes(("al", u[1])), E4M3, True, True)

            return emit

        def product(u, j):
            def emit(engine):
                nc.vector.scalar_tensor_tensor(
                    out=ds_tile(u)[:, j, :].rearrange("p (t q) -> p q t", t=4),
                    in0=tiles[("dk", u, j)][:].rearrange("p (q t) -> p q t", t=4),
                    scalar=1.0,
                    in1=k_tile(u)[:, j, :].rearrange("p (q t) -> p q t", t=4),
                    op0=MULT,
                    op1=MULT,
                    accum_out=row_parts[:, u[0], j, u[1] : u[1] + 1],
                )

            return emit

        def transpose(u, j):
            def emit(engine):
                tiles[("dsT", u, j)] = bank("tb")
                for t in range(4):
                    nc.tensor.transpose(tiles[("dsT", u, j)][:, cols(t)], ds_tile(u)[:, j, cols(t)], ident[:])

            return emit

        def transposed_copy(u, j):
            def emit(engine):
                nc.scalar.copy(out=grouped(("b",) + u)[:, cols(j), :], in_=tiles[("dsT", u, j)][:].rearrange("q (t p) -> q p t", t=4))

            return emit

        def add_up(u, t):
            def emit(engine):
                b = shared(("col", u), lambda: bank("col"))
                for j in range(4):
                    nc.tensor.matmul(b[:, cols(t)], lhsT=ds_tile(u)[:, j, cols(t)], rhs=ident[:], is_transpose=True, start=(j == 0), stop=(j == 3))

            return emit

        def column_sums(u):
            def emit(engine):
                nc.vector.tensor_reduce(out=col_parts[:, u[0], u[1], :], in_=tiles[("col", u)][:].rearrange("q (t p) -> q t p", t=4), axis=AXIS_X, op=ADD)

            return emit

        for i, u in enumerate(UNITS):
            g, h = u
            products = [("product", u, j) for j in range(4)]
            for j in range(4):
                task(("dk", u, j), [("T", 11)], dk(u, j), [("q", "g", g, j // 2), ("q", "al", h)], ("mm", ("dk", u, j)), rank=10 * i + 97, mode="mx")
                task(("product", u, j), [("V", 29)], product(u, j), [("dk", u, j), ("ld", "k", u, j // 2)], ("ds", u), ["mm", "k"] if j == 3 else ["mm"], 10 * i + 453)
                task(("dsT", u, j), [("T", 13)], transpose(u, j), [("product", u, j)], ("tb", (u, j)), rank=10 * i, mode="transpose")
                task(("copy", u, j), [("S", 23)], transposed_copy(u, j), [("dsT", u, j)], ("grp", ("b",) + u), ["tb"], 10 * i)
                task(("add", u, j), [("T", 13)], add_up(u, j), products, ("col", u), rank=10 * i - 257, mode="transpose")
            task(("q", "b") + u, [("V", 24)], quantise(("b",) + u, E5M2), [("copy", u, j) for j in range(4)], frees=["grp"], rank=10 * i - 650, port=True)
            task(("col", u), [("V", 23)], column_sums(u), [("add", u, t) for t in range(4)], frees=["col"], rank=10 * i + 366)
            operand(("a",) + u, lambda u=u: ds_tile(u), E5M2, products, 10 * i - 49, [("S", 46), ("G", 66)])
            readers = [("dsT", u, j) for j in range(4)] + [("add", u, t) for t in range(4)] + [("i", "a") + u + (n,) for n in range(PARTS)]
            task(("free", "ds", u), [("N", 0)], lambda engine: None, readers, frees=["ds"])

        def multiply(key):
            kind, i, j, f = key

            def emit(engine):
                tiles[key] = bank("mm")
                if kind == "dc":
                    for g in range(GROUPS):
                        mx(tiles[key], codes(("a", g, i)), cols(j), E5M2, codes(("x", g, f)), E4M3, g == 0, g == GROUPS - 1)
                else:
                    for h in range(CHUNKS):
                        mx(tiles[key], codes(("b", i, h)), cols(j), E5M2, codes(("c", h, f)), E4M3, h == 0, h == CHUNKS - 1)

            return emit

        def negated_col(h):
            nc.vector.scalar_tensor_tensor(out=minus_col[:, h, :], in0=col_parts[:, 0, h, :], scalar=-1.0, in1=col_parts[:, 1, h, :], op0=MULT, op1=SUBTRACT)
            return minus_col[:, h, :]

        def negated_row(g):
            nc.vector.tensor_reduce(out=minus_row[:, g, :], in_=row_parts[:, g, :, :], axis=AXIS_X, op=ADD)
            nc.vector.tensor_scalar(out=minus_row[:, g, :], in0=minus_row[:, g, :], scalar1=-1.0, scalar2=None, op0=MULT)
            return minus_row[:, g, :]

        def finish(key):
            kind, i, j, f = key

            def emit(engine):
                factor = shared(("minus", kind, i), lambda: negated_col(i) if kind == "dc" else negated_row(i))
                tiles[("out",) + key] = streamed("out", [P, 512], F32, SLOTS["out"])
                nc.vector.scalar_tensor_tensor(
                    out=tiles[("out",) + key][:],
                    in0=(c_raw if kind == "dc" else x_raw)[i][:, j, 512 * f : 512 * (f + 1)],
                    scalar=factor[:, j : j + 1],
                    in1=tiles[key][:],
                    op0=MULT,
                    op1=ADD,
                )

            return emit

        def store(key):
            kind, i, j, f = key
            dst = (dc_v if kind == "dc" else dx_v)[i, j, :, 512 * f : 512 * (f + 1)]
            return lambda engine: nc.sync.dma_start(out=dst, in_=tiles[("out",) + key][:])

        def gradient_tile(key, length, needs, rank, more):
            task(("mm", key), [("T", length)], multiply(key), needs, ("mm", key), rank=rank, mode="mx")
            task(("finish", key), [("V", 23)], finish(key), [("mm", key)] + more, ("out", key), ["mm"], rank)
            task(("store", key), [("Q", 22)], store(key), [("finish", key)], frees=["out"], rank=1000)

        for f in range(2):
            for j in range(4):
                for h in range(CHUNKS):
                    last = max(place[(g, h)] for g in range(GROUPS))
                    needs = [("q", "a", g, h) for g in range(GROUPS)] + [("q", "x", g, f) for g in range(GROUPS)]
                    sums = [("ld", "c", h)] + [("col", (g, h)) for g in range(GROUPS)]
                    gradient_tile(("dc", h, j, f), 22, needs, -1136 + 200 * last - 482 * f + j, sums)
                for g in range(GROUPS):
                    needs = [("q", "b", g, h) for h in range(CHUNKS)] + [("q", "c", h, f) for h in range(CHUNKS)]
                    gradient_tile(("dx", g, j, f), 44, needs, 38 + 1433 * g - 396 * f + j, [("ld", "x", g)])

        for name, engine in plan(tasks, SLOTS):
            tasks[name]["emit"](engine)
